import numpy as np
import ml_dtypes

BF16 = ml_dtypes.bfloat16


def bf(x):
    return np.asarray(x, np.float32).astype(BF16)


def f32(x):
    return np.asarray(x, np.float32)


def f64(x):
    return np.asarray(x).astype(np.float64)


def striped(idx):
    return np.tile(idx.reshape(-1, 16).T, (8, 1))


C, S, Q, K, H, N = 256, 512, 4, 128, 256, 512
NEG_SLOPE = 0.01
EPS = 1e-5


def lrelu(v):
    return np.maximum(v, NEG_SLOPE * v)


def layer_norm(v, gain, shift):
    mu = v.mean(axis=-1, keepdims=True)
    var = ((v - mu) ** 2).mean(axis=-1, keepdims=True)
    return (v - mu) / np.sqrt(var + EPS) * gain + shift


def row(scale, mean):
    return f32(mean + scale * np.random.standard_normal((Q * H,)))[None]


def setup_inputs():
    return {"x": f32(bf(np.random.standard_normal((C, S)))), "w1": bf(np.random.standard_normal((Q * K, H)) / np.sqrt(K)), "b1": row(0.1, 0.0), "gain1": row(0.1, 1.0), "shift1": row(0.1, 0.0), "w2": bf(np.random.standard_normal((Q * H, H)) / np.sqrt(H)), "b2": row(0.1, 0.0), "gain2": row(0.1, 1.0), "shift2": row(0.1, 0.0), "offs": striped(np.random.permutation(np.tile(np.arange(S), 2))[:N])}


def reference(x, w1, b1, gain1, shift1, w2, b2, gain2, shift2, offs):
    idx = offs[:16].T.reshape(-1)
    o = f64(x)[:, idx].reshape(C, Q, K)
    a1 = np.einsum('cqi,qit->cqt', o, f64(w1).reshape(Q, K, H)) + f64(b1).reshape(Q, H)[None]
    h1 = layer_norm(lrelu(a1), f64(gain1).reshape(Q, H)[None], f64(shift1).reshape(Q, H)[None])
    a2 = np.einsum('cqt,qtu->cqu', h1, f64(w2).reshape(Q, H, H)) + f64(b2).reshape(Q, H)[None]
    h2 = layer_norm(lrelu(a2), f64(gain2).reshape(Q, H)[None], f64(shift2).reshape(Q, H)[None])
    return h2.reshape(C, Q * H)

@@ -1,0 +1,156 @@
+import concourse.mybir as mybir
+from concourse.masks import make_identity
+
+F32, BF16, U16 = mybir.dt.float32, mybir.dt.bfloat16, mybir.dt.uint16
+ADD, SUB, MULT, MAX = (
+    mybir.AluOpType.add,
+    mybir.AluOpType.subtract,
+    mybir.AluOpType.mult,
+    mybir.AluOpType.max,
+)
+COPY = mybir.ActivationFunctionType.Copy
+IDENTITY = mybir.ActivationFunctionType.Identity
+SQRT = mybir.ActivationFunctionType.Sqrt
+
+P = 128
+C, S, Q, K, H, N = 256, 512, 4, 128, 256, 512
+CB = C // P
+TB = H // P
+PAIRS = Q // 2
+NEG_SLOPE = 0.01
+EPS = 1e-5
+FLOPS = 2 * C * Q * (K * H + H * H)
+
+
+def state_cols(q):
+    return slice(q * H, (q + 1) * H)
+
+
+def bias_lrelu_stats(nc, work, small, banks, bias_bc, eps):
+    a = work.tile([P, Q * H], F32, name="a")
+    v = work.tile([P, Q * H], F32, name="v")
+    for pair in range(PAIRS):
+        cols = slice(pair * 2 * H, (pair + 1) * 2 * H)
+        nc.vector.tensor_tensor(a[:, cols], banks[pair][:], bias_bc[:, cols], ADD)
+        nc.vector.scalar_tensor_tensor(v[:, cols], a[:, cols], NEG_SLOPE, a[:, cols], MULT, MAX)
+    stats = small.tile([P, Q, 6], F32, name="stats")
+    mean_var = small.tile([P, Q, 2], F32, name="mean_var")
+    for q in range(Q):
+        nc.vector.bn_stats(stats[:, q, :], v[:, state_cols(q)])
+        nc.vector.bn_aggr(mean_var[:, q, :], stats[:, q, :])
+    std = small.tile([P, Q], F32, name="std")
+    nc.scalar.activation(std[:], mean_var[:, :, 1], SQRT, bias=eps[:])
+    rstd = small.tile([P, Q], F32, name="rstd")
+    nc.vector.reciprocal(rstd[:], std[:])
+    return v, mean_var, rstd
+
+
+def tile_actor_dec_nw_kernel(tc, x, w1, b1, gain1, shift1, w2, b2, gain2, shift2, offs, out):
+    nc = tc.nc
+    with (
+        tc.tile_pool(name="held", bufs=1) as held,
+        tc.tile_pool(name="work", bufs=2) as work,
+        tc.tile_pool(name="small", bufs=4) as small,
+        tc.psum_pool(name="flip", bufs=2) as flip,
+        tc.psum_pool(name="acc", bufs=4) as acc,
+    ):
+        offsets = held.tile([P, N // 16], U16, name="offsets")
+        nc.sync.dma_start(offsets[:], offs)
+        x_blocks = []
+        for cb in range(CB):
+            x_block = held.tile([P, S], F32, name=f"x_block{cb}")
+            nc.sync.dma_start(x_block[:], x[cb * P : (cb + 1) * P, :])
+            x_blocks.append(x_block)
+
+        w1_sb = held.tile([P, Q, H], BF16, name="w1_sb")
+        nc.scalar.dma_start(w1_sb[:], w1.rearrange("(q i) t -> i q t", i=P))
+        w2_sb = held.tile([P, Q * TB, H], BF16, name="w2_sb")
+        nc.sync.dma_start(w2_sb[:], w2.rearrange("(k t) u -> t k u", t=P))
+
+        b1_bc = held.tile([P, Q * H], F32, name="b1_bc")
+        b2_bc = held.tile([P, Q * H], F32, name="b2_bc")
+        gain2_bc = held.tile([P, Q * H], F32, name="gain2_bc")
+        shift2_bc = held.tile([P, Q * H], F32, name="shift2_bc")
+        nc.scalar.dma_start(b1_bc[:], b1.rearrange("o n -> (o n)").partition_broadcast(P))
+        nc.scalar.dma_start(b2_bc[:], b2.rearrange("o n -> (o n)").partition_broadcast(P))
+        nc.gpsimd.dma_start(gain2_bc[:], gain2.rearrange("o n -> (o n)").partition_broadcast(P))
+        nc.gpsimd.dma_start(shift2_bc[:], shift2.rearrange("o n -> (o n)").partition_broadcast(P))
+
+        ident = held.tile([P, P], F32, name="ident")
+        make_identity(nc, ident[:])
+        eps = held.tile([P, 1], F32, name="eps")
+        nc.vector.memset(eps[:], EPS)
+
+        rows = held.tile([P, P], F32, name="rows")
+        nc.vector.memset(rows[:], 0.0)
+        nc.gpsimd.dma_start(rows[0 : Q * TB, :], gain1.rearrange("o (k t) -> (o k) t", t=P))
+        nc.gpsimd.dma_start(rows[Q * TB : 2 * Q * TB, :], shift1.rearrange("o (k t) -> (o k) t", t=P))
+        rows_ps = flip.tile([P, Q, P], F32, name="rows_ps", tag="oT_ps")
+        nc.tensor.transpose(rows_ps[:, 0, :], rows[:], ident[:])
+        cols1 = held.tile([P, 2 * Q * TB], F32, name="cols1")
+        nc.vector.tensor_copy(cols1[:], rows_ps[:, 0, 0 : 2 * Q * TB])
+        gain1_col = cols1[:, 0 : Q * TB]
+        shift1_col = cols1[:, Q * TB : 2 * Q * TB]
+
+        for cb in range(CB):
+            o = work.tile([P, N], F32, name="o")
+            nc.scalar.activation(o[:], x_blocks[cb][:].indirect(offsets[:]), COPY)
+
+            oT_ps = flip.tile([P, Q, P], F32, name="oT_ps")
+            for q in range(Q):
+                nc.tensor.transpose(oT_ps[:, q, :], o[:, q * K : (q + 1) * K], ident[:])
+            oT = work.tile([P, Q, P], BF16, name="oT")
+            nc.vector.tensor_copy(oT[:], oT_ps[:])
+
+            banks = []
+            for pair in range(PAIRS):
+                bank = acc.tile([P, 2 * H], F32, name="bank")
+                for j in range(2):
+                    q = 2 * pair + j
+                    nc.tensor.matmul(bank[:, j * H : (j + 1) * H], oT[:, q, :], w1_sb[:, q, :], start=True, stop=True)
+                banks.append(bank)
+            v, mean_var, rstd = bias_lrelu_stats(nc, work, small, banks, b1_bc, eps)
+
+            n = work.tile([P, Q * H], F32, name="n")
+            banks = []
+            for pair in range(PAIRS):
+                bank = acc.tile([P, 2 * H], F32, name="bank")
+                for j in range(2):
+                    q = 2 * pair + j
+                    nc.vector.tensor_scalar(
+                        n[:, state_cols(q)], v[:, state_cols(q)], mean_var[:, q, 0:1], rstd[:, q : q + 1], SUB, MULT
+                    )
+                    nT_ps = flip.tile([P, TB, P], F32, name="nT_ps")
+                    h1T = work.tile([P, TB, P], BF16, name="h1T")
+                    for tb in range(TB):
+                        k = q * TB + tb
+                        nc.tensor.transpose(nT_ps[:, tb, :], n[:, k * P : (k + 1) * P], ident[:])
+                        nc.scalar.activation(
+                            h1T[:, tb, :],
+                            nT_ps[:, tb, :],
+                            IDENTITY,
+                            bias=shift1_col[:, k : k + 1],
+                            scale=gain1_col[:, k : k + 1],
+                        )
+                    for tb in range(TB):
+                        nc.tensor.matmul(
+                            bank[:, j * H : (j + 1) * H],
+                            h1T[:, tb, :],
+                            w2_sb[:, q * TB + tb, :],
+                            start=(tb == 0),
+                            stop=(tb == TB - 1),
+                        )
+                banks.append(bank)
+            v, mean_var, rstd = bias_lrelu_stats(nc, work, small, banks, b2_bc, eps)
+
+            centred = work.tile([P, Q * H], F32, name="centred")
+            y = work.tile([P, Q * H], F32, name="y")
+            for q in range(Q):
+                cols = state_cols(q)
+                nc.vector.scalar_tensor_tensor(
+                    centred[:, cols], v[:, cols], mean_var[:, q, 0:1], gain2_bc[:, cols], SUB, MULT
+                )
+                nc.vector.scalar_tensor_tensor(
+                    y[:, cols], centred[:, cols], rstd[:, q : q + 1], shift2_bc[:, cols], MULT, ADD
+                )
+                nc.sync.dma_start(out[cb * P : (cb + 1) * P, cols], y[:, cols])

@@ -2,21 +2,16 @@ import concourse.mybir as mybir
 from concourse.masks import make_identity
 
 F32, BF16, U16 = mybir.dt.float32, mybir.dt.bfloat16, mybir.dt.uint16
-ADD, SUB, MULT, MAX = (
-    mybir.AluOpType.add,
-    mybir.AluOpType.subtract,
-    mybir.AluOpType.mult,
-    mybir.AluOpType.max,
-)
+ADD, MULT, MAX = mybir.AluOpType.add, mybir.AluOpType.mult, mybir.AluOpType.max
 COPY = mybir.ActivationFunctionType.Copy
 IDENTITY = mybir.ActivationFunctionType.Identity
+SQUARE = mybir.ActivationFunctionType.Square
 SQRT = mybir.ActivationFunctionType.Sqrt
 
 P = 128
 C, S, Q, K, H, N = 256, 512, 4, 128, 256, 512
 CB = C // P
 TB = H // P
-PAIRS = Q // 2
 NEG_SLOPE = 0.01
 EPS = 1e-5
 FLOPS = 2 * C * Q * (K * H + H * H)
@@ -26,131 +21,168 @@ def state_cols(q):
     return slice(q * H, (q + 1) * H)
 
 
-def bias_lrelu_stats(nc, work, small, banks, bias_bc, eps):
-    a = work.tile([P, Q * H], F32, name="a")
-    v = work.tile([P, Q * H], F32, name="v")
-    for pair in range(PAIRS):
-        cols = slice(pair * 2 * H, (pair + 1) * 2 * H)
-        nc.vector.tensor_tensor(a[:, cols], banks[pair][:], bias_bc[:, cols], ADD)
-        nc.vector.scalar_tensor_tensor(v[:, cols], a[:, cols], NEG_SLOPE, a[:, cols], MULT, MAX)
-    stats = small.tile([P, Q, 6], F32, name="stats")
-    mean_var = small.tile([P, Q, 2], F32, name="mean_var")
-    for q in range(Q):
-        nc.vector.bn_stats(stats[:, q, :], v[:, state_cols(q)])
-        nc.vector.bn_aggr(mean_var[:, q, :], stats[:, q, :])
-    std = small.tile([P, Q], F32, name="std")
-    nc.scalar.activation(std[:], mean_var[:, :, 1], SQRT, bias=eps[:])
-    rstd = small.tile([P, Q], F32, name="rstd")
-    nc.vector.reciprocal(rstd[:], std[:])
-    return v, mean_var, rstd
-
-
 def tile_actor_dec_nw_kernel(tc, x, w1, b1, gain1, shift1, w2, b2, gain2, shift2, offs, out):
     nc = tc.nc
     with (
         tc.tile_pool(name="held", bufs=1) as held,
-        tc.tile_pool(name="work", bufs=2) as work,
+        tc.tile_pool(name="work", bufs=4) as work,
         tc.tile_pool(name="small", bufs=4) as small,
-        tc.psum_pool(name="flip", bufs=2) as flip,
+        tc.psum_pool(name="flip_o", bufs=2) as flip_o,
+        tc.psum_pool(name="flip_n", bufs=2) as flip_n,
         tc.psum_pool(name="acc", bufs=4) as acc,
     ):
         offsets = held.tile([P, N // 16], U16, name="offsets")
-        nc.sync.dma_start(offsets[:], offs)
-        x_blocks = []
-        for cb in range(CB):
-            x_block = held.tile([P, S], F32, name=f"x_block{cb}")
-            nc.sync.dma_start(x_block[:], x[cb * P : (cb + 1) * P, :])
-            x_blocks.append(x_block)
-
+        x_blocks = [held.tile([P, S], F32, name=f"x_block{cb}") for cb in range(CB)]
         w1_sb = held.tile([P, Q, H], BF16, name="w1_sb")
-        nc.scalar.dma_start(w1_sb[:], w1.rearrange("(q i) t -> i q t", i=P))
         w2_sb = held.tile([P, Q * TB, H], BF16, name="w2_sb")
-        nc.sync.dma_start(w2_sb[:], w2.rearrange("(k t) u -> t k u", t=P))
-
         b1_bc = held.tile([P, Q * H], F32, name="b1_bc")
         b2_bc = held.tile([P, Q * H], F32, name="b2_bc")
         gain2_bc = held.tile([P, Q * H], F32, name="gain2_bc")
         shift2_bc = held.tile([P, Q * H], F32, name="shift2_bc")
-        nc.scalar.dma_start(b1_bc[:], b1.rearrange("o n -> (o n)").partition_broadcast(P))
-        nc.scalar.dma_start(b2_bc[:], b2.rearrange("o n -> (o n)").partition_broadcast(P))
-        nc.gpsimd.dma_start(gain2_bc[:], gain2.rearrange("o n -> (o n)").partition_broadcast(P))
-        nc.gpsimd.dma_start(shift2_bc[:], shift2.rearrange("o n -> (o n)").partition_broadcast(P))
+        rows = held.tile([P, P], F32, name="rows")
+        nc.vector.memset(rows[:], 0.0)
+
+        nc.sync.dma_start(offsets[:], offs)
+        nc.scalar.dma_start(x_blocks[0][:], x[0:P, :])
+        nc.sync.dma_start(x_blocks[1][:], x[P : 2 * P, :])
+        nc.sync.dma_start(w1_sb[:], w1.rearrange("(q i) t -> i q t", i=P))
+        nc.sync.dma_start(b1_bc[:], b1.rearrange("o n -> (o n)").partition_broadcast(P))
+        nc.sync.dma_start(rows[0 : Q * TB, :], gain1.rearrange("o (k t) -> (o k) t", t=P))
+        nc.sync.dma_start(rows[Q * TB : 2 * Q * TB, :], shift1.rearrange("o (k t) -> (o k) t", t=P))
+        nc.sync.dma_start(w2_sb[:], w2.rearrange("(k t) u -> t k u", t=P))
+        nc.sync.dma_start(b2_bc[:], b2.rearrange("o n -> (o n)").partition_broadcast(P))
+        nc.sync.dma_start(gain2_bc[:], gain2.rearrange("o n -> (o n)").partition_broadcast(P))
+        nc.sync.dma_start(shift2_bc[:], shift2.rearrange("o n -> (o n)").partition_broadcast(P))
 
         ident = held.tile([P, P], F32, name="ident")
         make_identity(nc, ident[:])
         eps = held.tile([P, 1], F32, name="eps")
         nc.vector.memset(eps[:], EPS)
+        warm = held.tile([P, 1], F32, name="warm")
+        nc.scalar.activation(warm[:], eps[:], SQRT)
 
-        rows = held.tile([P, P], F32, name="rows")
-        nc.vector.memset(rows[:], 0.0)
-        nc.gpsimd.dma_start(rows[0 : Q * TB, :], gain1.rearrange("o (k t) -> (o k) t", t=P))
-        nc.gpsimd.dma_start(rows[Q * TB : 2 * Q * TB, :], shift1.rearrange("o (k t) -> (o k) t", t=P))
-        rows_ps = flip.tile([P, Q, P], F32, name="rows_ps", tag="oT_ps")
-        nc.tensor.transpose(rows_ps[:, 0, :], rows[:], ident[:])
-        cols1 = held.tile([P, 2 * Q * TB], F32, name="cols1")
-        nc.vector.tensor_copy(cols1[:], rows_ps[:, 0, 0 : 2 * Q * TB])
-        gain1_col = cols1[:, 0 : Q * TB]
-        shift1_col = cols1[:, Q * TB : 2 * Q * TB]
 
-        for cb in range(CB):
-            o = work.tile([P, N], F32, name="o")
-            nc.scalar.activation(o[:], x_blocks[cb][:].indirect(offsets[:]), COPY)
+        def look_up_and_flip(q):
+            oT_ps = flip_o.tile([P, CB, P], F32, name="oT_ps")
+            for cb in range(CB):
+                o = work.tile([P, K], F32, name="o")
+                piece = offsets[:, q * (K // 16) : (q + 1) * (K // 16)]
+                nc.scalar.activation(o[:], x_blocks[cb][:].indirect(piece), COPY)
+                nc.tensor.transpose(oT_ps[:, cb, :], o[:], ident[:])
+            return oT_ps
 
-            oT_ps = flip.tile([P, Q, P], F32, name="oT_ps")
-            for q in range(Q):
-                nc.tensor.transpose(oT_ps[:, q, :], o[:, q * K : (q + 1) * K], ident[:])
-            oT = work.tile([P, Q, P], BF16, name="oT")
-            nc.vector.tensor_copy(oT[:], oT_ps[:])
+        def layer1(q, oT_ps):
+            oT = work.tile([P, CB, P], BF16, name="oT")
+            nc.scalar.activation(oT[:], oT_ps[:], COPY)
+            bank = acc.tile([P, CB, H], F32, name="bank")
+            for cb in range(CB):
+                nc.tensor.matmul(bank[:, cb, :], oT[:, cb, :], w1_sb[:, q, :], start=True, stop=True)
+            return bank
 
-            banks = []
-            for pair in range(PAIRS):
-                bank = acc.tile([P, 2 * H], F32, name="bank")
-                for j in range(2):
-                    q = 2 * pair + j
-                    nc.tensor.matmul(bank[:, j * H : (j + 1) * H], oT[:, q, :], w1_sb[:, q, :], start=True, stop=True)
-                banks.append(bank)
-            v, mean_var, rstd = bias_lrelu_stats(nc, work, small, banks, b1_bc, eps)
+        def lrelu_and_spread(bank, bias):
+            a = work.tile([P, CB, H], F32, name="a")
+            nc.vector.tensor_tensor(a[:], bank[:], bias.unsqueeze(1).to_broadcast([P, CB, H]), ADD)
+            v = work.tile([P, CB, H], F32, name="v")
+            total = small.tile([P, CB], F32, name="total")
+            for cb in range(CB):
+                nc.vector.scalar_tensor_tensor(
+                    v[:, cb, :], a[:, cb, :], NEG_SLOPE, a[:, cb, :], MULT, MAX, accum_out=total[:, cb : cb + 1]
+                )
+            neg_mean = small.tile([P, CB], F32, name="neg_mean")
+            nc.vector.tensor_scalar(neg_mean[:], total[:], -1.0 / H, None, MULT)
+            squares = work.tile([P, CB, H], F32, name="squares")
+            spread = small.tile([P, CB], F32, name="spread")
+            for cb in range(CB):
+                nc.scalar.activation(
+                    squares[:, cb, :],
+                    v[:, cb, :],
+                    SQUARE,
+                    bias=neg_mean[:, cb : cb + 1],
+                    accum_out=spread[:, cb : cb + 1],
+                )
+            std = small.tile([P, CB], F32, name="std")
+            nc.scalar.activation(std[:], spread[:], SQRT, bias=eps[:], scale=1.0 / H)
+            return v, neg_mean, std
 
-            n = work.tile([P, Q * H], F32, name="n")
-            banks = []
-            for pair in range(PAIRS):
-                bank = acc.tile([P, 2 * H], F32, name="bank")
-                for j in range(2):
-                    q = 2 * pair + j
-                    nc.vector.tensor_scalar(
-                        n[:, state_cols(q)], v[:, state_cols(q)], mean_var[:, q, 0:1], rstd[:, q : q + 1], SUB, MULT
+        def normalise_and_flip(v, neg_mean, std):
+            rstd = small.tile([P, CB], F32, name="rstd")
+            nc.vector.reciprocal(rstd[:], std[:])
+            nT_ps = flip_n.tile([P, TB, CB, P], F32, name="nT_ps")
+            n = work.tile([P, CB, H], F32, name="n")
+            for cb in range(CB):
+                nc.vector.tensor_scalar(
+                    n[:, cb, :], v[:, cb, :], neg_mean[:, cb : cb + 1], rstd[:, cb : cb + 1], ADD, MULT
+                )
+                for tb in range(TB):
+                    nc.tensor.transpose(nT_ps[:, tb, cb, :], n[:, cb, tb * P : (tb + 1) * P], ident[:])
+            return nT_ps
+
+        def gain1_shift1(q, nT_ps):
+            h1T = work.tile([P, TB, CB, P], BF16, name="h1T")
+            for tb in range(TB):
+                k = q * TB + tb
+                nc.scalar.activation(
+                    h1T[:, tb], nT_ps[:, tb], IDENTITY, bias=shift1_col[:, k : k + 1], scale=gain1_col[:, k : k + 1]
+                )
+            return h1T
+
+        def layer2(q, h1T):
+            bank = acc.tile([P, CB, H], F32, name="bank")
+            for cb in range(CB):
+                for tb in range(TB):
+                    nc.tensor.matmul(
+                        bank[:, cb, :],
+                        h1T[:, tb, cb, :],
+                        w2_sb[:, q * TB + tb, :],
+                        start=(tb == 0),
+                        stop=(tb == TB - 1),
                     )
-                    nT_ps = flip.tile([P, TB, P], F32, name="nT_ps")
-                    h1T = work.tile([P, TB, P], BF16, name="h1T")
-                    for tb in range(TB):
-                        k = q * TB + tb
-                        nc.tensor.transpose(nT_ps[:, tb, :], n[:, k * P : (k + 1) * P], ident[:])
-                        nc.scalar.activation(
-                            h1T[:, tb, :],
-                            nT_ps[:, tb, :],
-                            IDENTITY,
-                            bias=shift1_col[:, k : k + 1],
-                            scale=gain1_col[:, k : k + 1],
-                        )
-                    for tb in range(TB):
-                        nc.tensor.matmul(
-                            bank[:, j * H : (j + 1) * H],
-                            h1T[:, tb, :],
-                            w2_sb[:, q * TB + tb, :],
-                            start=(tb == 0),
-                            stop=(tb == TB - 1),
-                        )
-                banks.append(bank)
-            v, mean_var, rstd = bias_lrelu_stats(nc, work, small, banks, b2_bc, eps)
+            return bank
 
-            centred = work.tile([P, Q * H], F32, name="centred")
-            y = work.tile([P, Q * H], F32, name="y")
-            for q in range(Q):
-                cols = state_cols(q)
+        def centre_times_gain2(q, v, neg_mean):
+            centred = work.tile([P, CB, H], F32, name="centred")
+            for cb in range(CB):
                 nc.vector.scalar_tensor_tensor(
-                    centred[:, cols], v[:, cols], mean_var[:, q, 0:1], gain2_bc[:, cols], SUB, MULT
+                    centred[:, cb, :], v[:, cb, :], neg_mean[:, cb : cb + 1], gain2_bc[:, state_cols(q)], ADD, MULT
                 )
+            return centred
+
+        def scale_shift2_and_store(q, centred, std):
+            rstd = small.tile([P, CB], F32, name="rstd")
+            nc.vector.reciprocal(rstd[:], std[:])
+            y = work.tile([P, CB, H], F32, name="y")
+            for cb in range(CB):
                 nc.vector.scalar_tensor_tensor(
-                    y[:, cols], centred[:, cols], rstd[:, q : q + 1], shift2_bc[:, cols], MULT, ADD
+                    y[:, cb, :], centred[:, cb, :], rstd[:, cb : cb + 1], shift2_bc[:, state_cols(q)], MULT, ADD
                 )
-                nc.sync.dma_start(out[cb * P : (cb + 1) * P, cols], y[:, cols])
+                nc.sync.dma_start(out[cb * P : (cb + 1) * P, state_cols(q)], y[:, cb, :])
+
+        flipped_o, bank1 = {}, {}
+        for q in range(Q + 1):
+            if q < Q:
+                flipped_o[q] = look_up_and_flip(q)
+            if q >= 1:
+                bank1[q - 1] = layer1(q - 1, flipped_o[q - 1])
+
+        started, flipped_n, bank2 = {}, {}, {}
+        for r in range(2 * Q + 1):
+            if r == 2:
+                rows_ps = flip_o.tile([P, CB, P], F32, name="rows_ps", tag="oT_ps")
+                nc.tensor.transpose(rows_ps[:, 0, :], rows[:], ident[:])
+                cols1 = held.tile([P, 2 * Q * TB], F32, name="cols1")
+                nc.scalar.activation(cols1[:], rows_ps[:, 0, 0 : 2 * Q * TB], COPY)
+                gain1_col = cols1[:, 0 : Q * TB]
+                shift1_col = cols1[:, Q * TB : 2 * Q * TB]
+            if 2 <= r < Q + 2:
+                h1T = gain1_shift1(r - 2, flipped_n[r - 2])
+            if r < Q:
+                started[r] = lrelu_and_spread(bank1[r], b1_bc[:, state_cols(r)])
+            elif r < 2 * Q:
+                v, neg_mean, std = lrelu_and_spread(bank2[r - Q], b2_bc[:, state_cols(r - Q)])
+                started[r] = (centre_times_gain2(r - Q, v, neg_mean), std)
+            if 1 <= r <= Q:
+                flipped_n[r - 1] = normalise_and_flip(*started[r - 1])
+            elif r > Q:
+                scale_shift2_and_store(r - 1 - Q, *started[r - 1])
+            if 2 <= r < Q + 2:
+                bank2[r - 2] = layer2(r - 2, h1T)

@@ -45,10 +45,8 @@ def tile_actor_dec_nw_kernel(tc, x, w1, b1, gain1, shift1, w2, b2, gain2, shift2
         nc.sync.dma_start(offsets[:], offs)
         nc.scalar.dma_start(x_blocks[0][:], x[0:P, :])
         nc.sync.dma_start(x_blocks[1][:], x[P : 2 * P, :])
-        nc.sync.dma_start(w1_sb[:], w1.rearrange("(q i) t -> i q t", i=P))
+        nc.scalar.dma_start(w1_sb[:], w1.rearrange("(q i) t -> i q t", i=P))
         nc.sync.dma_start(b1_bc[:], b1.rearrange("o n -> (o n)").partition_broadcast(P))
-        nc.sync.dma_start(rows[0 : Q * TB, :], gain1.rearrange("o (k t) -> (o k) t", t=P))
-        nc.sync.dma_start(rows[Q * TB : 2 * Q * TB, :], shift1.rearrange("o (k t) -> (o k) t", t=P))
         nc.sync.dma_start(w2_sb[:], w2.rearrange("(k t) u -> t k u", t=P))
         nc.sync.dma_start(b2_bc[:], b2.rearrange("o n -> (o n)").partition_broadcast(P))
         nc.sync.dma_start(gain2_bc[:], gain2.rearrange("o n -> (o n)").partition_broadcast(P))
@@ -56,6 +54,8 @@ def tile_actor_dec_nw_kernel(tc, x, w1, b1, gain1, shift1, w2, b2, gain2, shift2
 
         ident = held.tile([P, P], F32, name="ident")
         make_identity(nc, ident[:])
+        nc.gpsimd.dma_start(rows[0 : Q * TB, :], gain1.rearrange("o (k t) -> (o k) t", t=P))
+        nc.gpsimd.dma_start(rows[Q * TB : 2 * Q * TB, :], shift1.rearrange("o (k t) -> (o k) t", t=P))
         eps = held.tile([P, 1], F32, name="eps")
         nc.vector.memset(eps[:], EPS)
         warm = held.tile([P, 1], F32, name="warm")
@@ -81,15 +81,14 @@ def tile_actor_dec_nw_kernel(tc, x, w1, b1, gain1, shift1, w2, b2, gain2, shift2
 
         def lrelu_and_spread(bank, bias):
             a = work.tile([P, CB, H], F32, name="a")
-            nc.vector.tensor_tensor(a[:], bank[:], bias.unsqueeze(1).to_broadcast([P, CB, H]), ADD)
+            for cb in range(CB):
+                nc.vector.tensor_tensor(a[:, cb, :], bank[:, cb, :], bias, ADD)
             v = work.tile([P, CB, H], F32, name="v")
             total = small.tile([P, CB], F32, name="total")
             for cb in range(CB):
                 nc.vector.scalar_tensor_tensor(
                     v[:, cb, :], a[:, cb, :], NEG_SLOPE, a[:, cb, :], MULT, MAX, accum_out=total[:, cb : cb + 1]
                 )
-            neg_mean = small.tile([P, CB], F32, name="neg_mean")
-            nc.vector.tensor_scalar(neg_mean[:], total[:], -1.0 / H, None, MULT)
             squares = work.tile([P, CB, H], F32, name="squares")
             spread = small.tile([P, CB], F32, name="spread")
             for cb in range(CB):
@@ -97,16 +96,25 @@ def tile_actor_dec_nw_kernel(tc, x, w1, b1, gain1, shift1, w2, b2, gain2, shift2
                     squares[:, cb, :],
                     v[:, cb, :],
                     SQUARE,
-                    bias=neg_mean[:, cb : cb + 1],
+                    bias=total[:, cb : cb + 1],
+                    scale=-float(H),
                     accum_out=spread[:, cb : cb + 1],
                 )
             std = small.tile([P, CB], F32, name="std")
-            nc.scalar.activation(std[:], spread[:], SQRT, bias=eps[:], scale=1.0 / H)
-            return v, neg_mean, std
+            nc.scalar.activation(std[:], spread[:], SQRT, bias=eps[:], scale=1.0 / H**3)
+            return v, total, std
 
-        def normalise_and_flip(v, neg_mean, std):
+        def one_over(std):
             rstd = small.tile([P, CB], F32, name="rstd")
             nc.vector.reciprocal(rstd[:], std[:])
+            return rstd
+
+        def minus_mean(total):
+            neg_mean = small.tile([P, CB], F32, name="neg_mean")
+            nc.vector.tensor_scalar(neg_mean[:], total[:], -1.0 / H, None, MULT)
+            return neg_mean
+
+        def normalise_and_flip(v, neg_mean, rstd):
             nT_ps = flip_n.tile([P, TB, CB, P], F32, name="nT_ps")
             n = work.tile([P, CB, H], F32, name="n")
             for cb in range(CB):
@@ -117,16 +125,13 @@ def tile_actor_dec_nw_kernel(tc, x, w1, b1, gain1, shift1, w2, b2, gain2, shift2
                     nc.tensor.transpose(nT_ps[:, tb, cb, :], n[:, cb, tb * P : (tb + 1) * P], ident[:])
             return nT_ps
 
-        def gain1_shift1(q, nT_ps):
+        def layer2(q, nT_ps):
             h1T = work.tile([P, TB, CB, P], BF16, name="h1T")
             for tb in range(TB):
                 k = q * TB + tb
                 nc.scalar.activation(
                     h1T[:, tb], nT_ps[:, tb], IDENTITY, bias=shift1_col[:, k : k + 1], scale=gain1_col[:, k : k + 1]
                 )
-            return h1T
-
-        def layer2(q, h1T):
             bank = acc.tile([P, CB, H], F32, name="bank")
             for cb in range(CB):
                 for tb in range(TB):
@@ -147,9 +152,7 @@ def tile_actor_dec_nw_kernel(tc, x, w1, b1, gain1, shift1, w2, b2, gain2, shift2
                 )
             return centred
 
-        def scale_shift2_and_store(q, centred, std):
-            rstd = small.tile([P, CB], F32, name="rstd")
-            nc.vector.reciprocal(rstd[:], std[:])
+        def scale_shift2_and_store(q, centred, rstd):
             y = work.tile([P, CB, H], F32, name="y")
             for cb in range(CB):
                 nc.vector.scalar_tensor_tensor(
@@ -157,32 +160,40 @@ def tile_actor_dec_nw_kernel(tc, x, w1, b1, gain1, shift1, w2, b2, gain2, shift2
                 )
                 nc.sync.dma_start(out[cb * P : (cb + 1) * P, state_cols(q)], y[:, cb, :])
 
-        flipped_o, bank1 = {}, {}
+        flipped_o, bank1, bank2 = {}, {}, {}
         for q in range(Q + 1):
             if q < Q:
                 flipped_o[q] = look_up_and_flip(q)
             if q >= 1:
                 bank1[q - 1] = layer1(q - 1, flipped_o[q - 1])
 
-        started, flipped_n, bank2 = {}, {}, {}
-        for r in range(2 * Q + 1):
-            if r == 2:
+        started = {}
+        for q in range(Q + 1):
+            if q < Q:
+                started[q] = lrelu_and_spread(bank1[q], b1_bc[:, state_cols(q)])
+            else:
+                started[q] = lrelu_and_spread(bank2[0], b2_bc[:, state_cols(0)])
+            if q == 1:
                 rows_ps = flip_o.tile([P, CB, P], F32, name="rows_ps", tag="oT_ps")
                 nc.tensor.transpose(rows_ps[:, 0, :], rows[:], ident[:])
                 cols1 = held.tile([P, 2 * Q * TB], F32, name="cols1")
                 nc.scalar.activation(cols1[:], rows_ps[:, 0, 0 : 2 * Q * TB], COPY)
                 gain1_col = cols1[:, 0 : Q * TB]
                 shift1_col = cols1[:, Q * TB : 2 * Q * TB]
-            if 2 <= r < Q + 2:
-                h1T = gain1_shift1(r - 2, flipped_n[r - 2])
-            if r < Q:
-                started[r] = lrelu_and_spread(bank1[r], b1_bc[:, state_cols(r)])
-            elif r < 2 * Q:
-                v, neg_mean, std = lrelu_and_spread(bank2[r - Q], b2_bc[:, state_cols(r - Q)])
-                started[r] = (centre_times_gain2(r - Q, v, neg_mean), std)
-            if 1 <= r <= Q:
-                flipped_n[r - 1] = normalise_and_flip(*started[r - 1])
-            elif r > Q:
-                scale_shift2_and_store(r - 1 - Q, *started[r - 1])
-            if 2 <= r < Q + 2:
-                bank2[r - 2] = layer2(r - 2, h1T)
+            if q >= 1:
+                v, total, std = started[q - 1]
+                bank2[q - 1] = layer2(q - 1, normalise_and_flip(v, minus_mean(total), one_over(std)))
+
+        previous = None
+        for q in range(Q + 1):
+            if 1 <= q < Q:
+                started[Q + q] = lrelu_and_spread(bank2[q], b2_bc[:, state_cols(q)])
+            if previous is not None:
+                rstd = one_over(previous[1])
+            if q < Q:
+                v, total, std = started[Q + q]
+                neg_mean = minus_mean(total)
+            if previous is not None:
+                scale_shift2_and_store(q - 1, previous[0], rstd)
+            if q < Q:
+                previous = (centre_times_gain2(q, v, neg_mean), std)

@@ -6,7 +6,7 @@ ADD, MULT, MAX = mybir.AluOpType.add, mybir.AluOpType.mult, mybir.AluOpType.max
 COPY = mybir.ActivationFunctionType.Copy
 IDENTITY = mybir.ActivationFunctionType.Identity
 SQUARE = mybir.ActivationFunctionType.Square
-SQRT = mybir.ActivationFunctionType.Sqrt
+RSQRT = mybir.ActivationFunctionType.Abs_reciprocal_sqrt
 
 P = 128
 C, S, Q, K, H, N = 256, 512, 4, 128, 256, 512
@@ -15,6 +15,7 @@ TB = H // P
 NEG_SLOPE = 0.01
 EPS = 1e-5
 FLOPS = 2 * C * Q * (K * H + H * H)
+PE_WARM_UP = 4
 
 
 def state_cols(q):
@@ -47,6 +48,8 @@ def tile_actor_dec_nw_kernel(tc, x, w1, b1, gain1, shift1, w2, b2, gain2, shift2
         nc.sync.dma_start(x_blocks[1][:], x[P : 2 * P, :])
         nc.scalar.dma_start(w1_sb[:], w1.rearrange("(q i) t -> i q t", i=P))
         nc.sync.dma_start(b1_bc[:], b1.rearrange("o n -> (o n)").partition_broadcast(P))
+        nc.sync.dma_start(rows[0 : Q * TB, :], gain1.rearrange("o (k t) -> (o k) t", t=P))
+        nc.sync.dma_start(rows[Q * TB : 2 * Q * TB, :], shift1.rearrange("o (k t) -> (o k) t", t=P))
         nc.sync.dma_start(w2_sb[:], w2.rearrange("(k t) u -> t k u", t=P))
         nc.sync.dma_start(b2_bc[:], b2.rearrange("o n -> (o n)").partition_broadcast(P))
         nc.sync.dma_start(gain2_bc[:], gain2.rearrange("o n -> (o n)").partition_broadcast(P))
@@ -54,12 +57,13 @@ def tile_actor_dec_nw_kernel(tc, x, w1, b1, gain1, shift1, w2, b2, gain2, shift2
 
         ident = held.tile([P, P], F32, name="ident")
         make_identity(nc, ident[:])
-        nc.gpsimd.dma_start(rows[0 : Q * TB, :], gain1.rearrange("o (k t) -> (o k) t", t=P))
-        nc.gpsimd.dma_start(rows[Q * TB : 2 * Q * TB, :], shift1.rearrange("o (k t) -> (o k) t", t=P))
+        warm_ps = flip_n.tile([P, TB, CB, P], F32, name="warm_ps", tag="nT_ps")
+        for i in range(PE_WARM_UP):
+            nc.tensor.matmul(warm_ps[:, 0, 0, :], ident[:], ident[:], start=True, stop=True)
         eps = held.tile([P, 1], F32, name="eps")
         nc.vector.memset(eps[:], EPS)
         warm = held.tile([P, 1], F32, name="warm")
-        nc.scalar.activation(warm[:], eps[:], SQRT)
+        nc.scalar.activation(warm[:], eps[:], RSQRT)
 
 
         def look_up_and_flip(q):
@@ -100,14 +104,9 @@ def tile_actor_dec_nw_kernel(tc, x, w1, b1, gain1, shift1, w2, b2, gain2, shift2
                     scale=-float(H),
                     accum_out=spread[:, cb : cb + 1],
                 )
-            std = small.tile([P, CB], F32, name="std")
-            nc.scalar.activation(std[:], spread[:], SQRT, bias=eps[:], scale=1.0 / H**3)
-            return v, total, std
-
-        def one_over(std):
             rstd = small.tile([P, CB], F32, name="rstd")
-            nc.vector.reciprocal(rstd[:], std[:])
-            return rstd
+            nc.scalar.activation(rstd[:], spread[:], RSQRT, bias=eps[:], scale=1.0 / H**3)
+            return v, total, rstd
 
         def minus_mean(total):
             neg_mean = small.tile([P, CB], F32, name="neg_mean")
@@ -158,7 +157,8 @@ def tile_actor_dec_nw_kernel(tc, x, w1, b1, gain1, shift1, w2, b2, gain2, shift2
                 nc.vector.scalar_tensor_tensor(
                     y[:, cb, :], centred[:, cb, :], rstd[:, cb : cb + 1], shift2_bc[:, state_cols(q)], MULT, ADD
                 )
-                nc.sync.dma_start(out[cb * P : (cb + 1) * P, state_cols(q)], y[:, cb, :])
+                store_queue = (nc.sync, nc.scalar)[cb]
+                store_queue.dma_start(out[cb * P : (cb + 1) * P, state_cols(q)], y[:, cb, :])
 
         flipped_o, bank1, bank2 = {}, {}, {}
         for q in range(Q + 1):
@@ -181,19 +181,17 @@ def tile_actor_dec_nw_kernel(tc, x, w1, b1, gain1, shift1, w2, b2, gain2, shift2
                 gain1_col = cols1[:, 0 : Q * TB]
                 shift1_col = cols1[:, Q * TB : 2 * Q * TB]
             if q >= 1:
-                v, total, std = started[q - 1]
-                bank2[q - 1] = layer2(q - 1, normalise_and_flip(v, minus_mean(total), one_over(std)))
+                v, total, rstd = started[q - 1]
+                bank2[q - 1] = layer2(q - 1, normalise_and_flip(v, minus_mean(total), rstd))
 
         previous = None
         for q in range(Q + 1):
             if 1 <= q < Q:
                 started[Q + q] = lrelu_and_spread(bank2[q], b2_bc[:, state_cols(q)])
-            if previous is not None:
-                rstd = one_over(previous[1])
             if q < Q:
-                v, total, std = started[Q + q]
+                v, total, rstd = started[Q + q]
                 neg_mean = minus_mean(total)
             if previous is not None:
-                scale_shift2_and_store(q - 1, previous[0], rstd)
+                scale_shift2_and_store(q - 1, *previous)
             if q < Q:
-                previous = (centre_times_gain2(q, v, neg_mean), std)
+                previous = (centre_times_gain2(q, v, neg_mean), rstd)

@@ -15,7 +15,6 @@ TB = H // P
 NEG_SLOPE = 0.01
 EPS = 1e-5
 FLOPS = 2 * C * Q * (K * H + H * H)
-PE_WARM_UP = 4
 
 
 def state_cols(q):
@@ -57,9 +56,6 @@ def tile_actor_dec_nw_kernel(tc, x, w1, b1, gain1, shift1, w2, b2, gain2, shift2
 
         ident = held.tile([P, P], F32, name="ident")
         make_identity(nc, ident[:])
-        warm_ps = flip_n.tile([P, TB, CB, P], F32, name="warm_ps", tag="nT_ps")
-        for i in range(PE_WARM_UP):
-            nc.tensor.matmul(warm_ps[:, 0, 0, :], ident[:], ident[:], start=True, stop=True)
         eps = held.tile([P, 1], F32, name="eps")
         nc.vector.memset(eps[:], EPS)
         warm = held.tile([P, 1], F32, name="warm")
@@ -83,10 +79,13 @@ def tile_actor_dec_nw_kernel(tc, x, w1, b1, gain1, shift1, w2, b2, gain2, shift2
                 nc.tensor.matmul(bank[:, cb, :], oT[:, cb, :], w1_sb[:, q, :], start=True, stop=True)
             return bank
 
-        def lrelu_and_spread(bank, bias):
+        def add_bias(bank, bias):
             a = work.tile([P, CB, H], F32, name="a")
             for cb in range(CB):
                 nc.vector.tensor_tensor(a[:, cb, :], bank[:, cb, :], bias, ADD)
+            return a
+
+        def lrelu_and_spread(a):
             v = work.tile([P, CB, H], F32, name="v")
             total = small.tile([P, CB], F32, name="total")
             for cb in range(CB):
@@ -113,7 +112,7 @@ def tile_actor_dec_nw_kernel(tc, x, w1, b1, gain1, shift1, w2, b2, gain2, shift2
             nc.vector.tensor_scalar(neg_mean[:], total[:], -1.0 / H, None, MULT)
             return neg_mean
 
-        def normalise_and_flip(v, neg_mean, rstd):
+        def norm1_and_layer2(q, v, neg_mean, rstd):
             nT_ps = flip_n.tile([P, TB, CB, P], F32, name="nT_ps")
             n = work.tile([P, CB, H], F32, name="n")
             for cb in range(CB):
@@ -122,9 +121,6 @@ def tile_actor_dec_nw_kernel(tc, x, w1, b1, gain1, shift1, w2, b2, gain2, shift2
                 )
                 for tb in range(TB):
                     nc.tensor.transpose(nT_ps[:, tb, cb, :], n[:, cb, tb * P : (tb + 1) * P], ident[:])
-            return nT_ps
-
-        def layer2(q, nT_ps):
             h1T = work.tile([P, TB, CB, P], BF16, name="h1T")
             for tb in range(TB):
                 k = q * TB + tb
@@ -143,55 +139,44 @@ def tile_actor_dec_nw_kernel(tc, x, w1, b1, gain1, shift1, w2, b2, gain2, shift2
                     )
             return bank
 
-        def centre_times_gain2(q, v, neg_mean):
+        def norm2_and_store(q, v, neg_mean, rstd):
             centred = work.tile([P, CB, H], F32, name="centred")
             for cb in range(CB):
                 nc.vector.scalar_tensor_tensor(
                     centred[:, cb, :], v[:, cb, :], neg_mean[:, cb : cb + 1], gain2_bc[:, state_cols(q)], ADD, MULT
                 )
-            return centred
-
-        def scale_shift2_and_store(q, centred, rstd):
             y = work.tile([P, CB, H], F32, name="y")
             for cb in range(CB):
                 nc.vector.scalar_tensor_tensor(
                     y[:, cb, :], centred[:, cb, :], rstd[:, cb : cb + 1], shift2_bc[:, state_cols(q)], MULT, ADD
                 )
-                store_queue = (nc.sync, nc.scalar)[cb]
-                store_queue.dma_start(out[cb * P : (cb + 1) * P, state_cols(q)], y[:, cb, :])
+                nc.sync.dma_start(out[cb * P : (cb + 1) * P, state_cols(q)], y[:, cb, :])
 
-        flipped_o, bank1, bank2 = {}, {}, {}
+        flipped_o = {}
+        banks = {}
         for q in range(Q + 1):
             if q < Q:
                 flipped_o[q] = look_up_and_flip(q)
             if q >= 1:
-                bank1[q - 1] = layer1(q - 1, flipped_o[q - 1])
+                banks[q - 1] = layer1(q - 1, flipped_o[q - 1])
 
-        started = {}
-        for q in range(Q + 1):
-            if q < Q:
-                started[q] = lrelu_and_spread(bank1[q], b1_bc[:, state_cols(q)])
-            else:
-                started[q] = lrelu_and_spread(bank2[0], b2_bc[:, state_cols(0)])
-            if q == 1:
+        biases = (b1_bc, b2_bc)
+        for j in range(2 * Q + 1):
+            if j < 2 * Q:
+                a = add_bias(banks[j], biases[j // Q][:, state_cols(j % Q)])
+            if j >= 1:
+                neg_mean = minus_mean(total)
+                previous = (v, neg_mean, rstd)
+            if j < 2 * Q:
+                v, total, rstd = lrelu_and_spread(a)
+            if j == 1:
                 rows_ps = flip_o.tile([P, CB, P], F32, name="rows_ps", tag="oT_ps")
                 nc.tensor.transpose(rows_ps[:, 0, :], rows[:], ident[:])
                 cols1 = held.tile([P, 2 * Q * TB], F32, name="cols1")
                 nc.scalar.activation(cols1[:], rows_ps[:, 0, 0 : 2 * Q * TB], COPY)
                 gain1_col = cols1[:, 0 : Q * TB]
                 shift1_col = cols1[:, Q * TB : 2 * Q * TB]
-            if q >= 1:
-                v, total, rstd = started[q - 1]
-                bank2[q - 1] = layer2(q - 1, normalise_and_flip(v, minus_mean(total), rstd))
-
-        previous = None
-        for q in range(Q + 1):
-            if 1 <= q < Q:
-                started[Q + q] = lrelu_and_spread(bank2[q], b2_bc[:, state_cols(q)])
-            if q < Q:
-                v, total, rstd = started[Q + q]
-                neg_mean = minus_mean(total)
-            if previous is not None:
-                scale_shift2_and_store(q - 1, *previous)
-            if q < Q:
-                previous = (centre_times_gain2(q, v, neg_mean), rstd)
+            if 1 <= j <= Q:
+                banks[Q + j - 1] = norm1_and_layer2(j - 1, *previous)
+            elif j > Q:
+                norm2_and_store(j - 1 - Q, *previous)

@@ -36,7 +36,6 @@ def tile_actor_dec_nw_kernel(tc, x, w1, b1, gain1, shift1, w2, b2, gain2, shift2
         w1_sb = held.tile([P, Q, H], BF16, name="w1_sb")
         w2_sb = held.tile([P, Q * TB, H], BF16, name="w2_sb")
         b1_bc = held.tile([P, Q * H], F32, name="b1_bc")
-        b2_bc = held.tile([P, Q * H], F32, name="b2_bc")
         gain2_bc = held.tile([P, Q * H], F32, name="gain2_bc")
         shift2_bc = held.tile([P, Q * H], F32, name="shift2_bc")
         rows = held.tile([P, P], F32, name="rows")
@@ -49,8 +48,8 @@ def tile_actor_dec_nw_kernel(tc, x, w1, b1, gain1, shift1, w2, b2, gain2, shift2
         nc.sync.dma_start(b1_bc[:], b1.rearrange("o n -> (o n)").partition_broadcast(P))
         nc.sync.dma_start(rows[0 : Q * TB, :], gain1.rearrange("o (k t) -> (o k) t", t=P))
         nc.sync.dma_start(rows[Q * TB : 2 * Q * TB, :], shift1.rearrange("o (k t) -> (o k) t", t=P))
+        nc.sync.dma_start(rows[2 * Q * TB : 3 * Q * TB, :], b2.rearrange("o (k t) -> (o k) t", t=P))
         nc.sync.dma_start(w2_sb[:], w2.rearrange("(k t) u -> t k u", t=P))
-        nc.sync.dma_start(b2_bc[:], b2.rearrange("o n -> (o n)").partition_broadcast(P))
         nc.sync.dma_start(gain2_bc[:], gain2.rearrange("o n -> (o n)").partition_broadcast(P))
         nc.sync.dma_start(shift2_bc[:], shift2.rearrange("o n -> (o n)").partition_broadcast(P))
 
@@ -85,12 +84,17 @@ def tile_actor_dec_nw_kernel(tc, x, w1, b1, gain1, shift1, w2, b2, gain2, shift2
                 nc.vector.tensor_tensor(a[:, cb, :], bank[:, cb, :], bias, ADD)
             return a
 
-        def lrelu_and_spread(a):
+        def times_slope(bank):
+            sloped = work.tile([P, CB, H], F32, name="sloped")
+            nc.scalar.activation(sloped[:], bank[:], COPY, scale=NEG_SLOPE)
+            return sloped
+
+        def lrelu_and_spread(a, slope, other):
             v = work.tile([P, CB, H], F32, name="v")
             total = small.tile([P, CB], F32, name="total")
             for cb in range(CB):
                 nc.vector.scalar_tensor_tensor(
-                    v[:, cb, :], a[:, cb, :], NEG_SLOPE, a[:, cb, :], MULT, MAX, accum_out=total[:, cb : cb + 1]
+                    v[:, cb, :], a[:, cb, :], slope, other[:, cb, :], MULT, MAX, accum_out=total[:, cb : cb + 1]
                 )
             squares = work.tile([P, CB, H], F32, name="squares")
             spread = small.tile([P, CB], F32, name="spread")
@@ -129,13 +133,24 @@ def tile_actor_dec_nw_kernel(tc, x, w1, b1, gain1, shift1, w2, b2, gain2, shift2
                 )
             bank = acc.tile([P, CB, H], F32, name="bank")
             for cb in range(CB):
+                for ub in range(TB):
+                    k = q * TB + ub
+                    nc.tensor.matmul(
+                        bank[:, cb, ub * P : (ub + 1) * P],
+                        b2_col[:, k : k + 1].to_broadcast([P, P]),
+                        ident[:],
+                        is_transpose=True,
+                        start=(cb == 0 and ub == 0),
+                        stop=False,
+                    )
+            for cb in range(CB):
                 for tb in range(TB):
                     nc.tensor.matmul(
                         bank[:, cb, :],
                         h1T[:, tb, cb, :],
                         w2_sb[:, q * TB + tb, :],
-                        start=(tb == 0),
-                        stop=(tb == TB - 1),
+                        start=False,
+                        stop=(cb == CB - 1 and tb == TB - 1),
                     )
             return bank
 
@@ -160,22 +175,27 @@ def tile_actor_dec_nw_kernel(tc, x, w1, b1, gain1, shift1, w2, b2, gain2, shift2
             if q >= 1:
                 banks[q - 1] = layer1(q - 1, flipped_o[q - 1])
 
-        biases = (b1_bc, b2_bc)
+        sloped = {}
         for j in range(2 * Q + 1):
-            if j < 2 * Q:
-                a = add_bias(banks[j], biases[j // Q][:, state_cols(j % Q)])
+            if j < Q:
+                a = add_bias(banks[j], b1_bc[:, state_cols(j)])
             if j >= 1:
                 neg_mean = minus_mean(total)
                 previous = (v, neg_mean, rstd)
-            if j < 2 * Q:
-                v, total, rstd = lrelu_and_spread(a)
+            if j < Q:
+                v, total, rstd = lrelu_and_spread(a, NEG_SLOPE, a)
+            elif j < 2 * Q:
+                v, total, rstd = lrelu_and_spread(banks[j], 1.0, sloped[j])
+            if Q <= j + 1 < 2 * Q:
+                sloped[j + 1] = times_slope(banks[j + 1])
             if j == 1:
                 rows_ps = flip_o.tile([P, CB, P], F32, name="rows_ps", tag="oT_ps")
                 nc.tensor.transpose(rows_ps[:, 0, :], rows[:], ident[:])
-                cols1 = held.tile([P, 2 * Q * TB], F32, name="cols1")
-                nc.scalar.activation(cols1[:], rows_ps[:, 0, 0 : 2 * Q * TB], COPY)
+                cols1 = held.tile([P, 3 * Q * TB], F32, name="cols1")
+                nc.scalar.activation(cols1[:], rows_ps[:, 0, 0 : 3 * Q * TB], COPY)
                 gain1_col = cols1[:, 0 : Q * TB]
                 shift1_col = cols1[:, Q * TB : 2 * Q * TB]
+                b2_col = cols1[:, 2 * Q * TB : 3 * Q * TB]
             if 1 <= j <= Q:
                 banks[Q + j - 1] = norm1_and_layer2(j - 1, *previous)
             elif j > Q:

@@ -15,6 +15,7 @@ TB = H // P
 NEG_SLOPE = 0.01
 EPS = 1e-5
 FLOPS = 2 * C * Q * (K * H + H * H)
+BEHIND = 2
 
 
 def state_cols(q):
@@ -61,27 +62,25 @@ def tile_actor_dec_nw_kernel(tc, x, w1, b1, gain1, shift1, w2, b2, gain2, shift2
         nc.scalar.activation(warm[:], eps[:], RSQRT)
 
 
-        def look_up_and_flip(q):
-            oT_ps = flip_o.tile([P, CB, P], F32, name="oT_ps")
-            for cb in range(CB):
-                o = work.tile([P, K], F32, name="o")
-                piece = offsets[:, q * (K // 16) : (q + 1) * (K // 16)]
-                nc.scalar.activation(o[:], x_blocks[cb][:].indirect(piece), COPY)
-                nc.tensor.transpose(oT_ps[:, cb, :], o[:], ident[:])
+        def look_up_and_flip(q, cb):
+            o = work.tile([P, K], F32, name="o")
+            piece = offsets[:, q * (K // 16) : (q + 1) * (K // 16)]
+            nc.scalar.activation(o[:], x_blocks[cb][:].indirect(piece), COPY)
+            oT_ps = flip_o.tile([P, P], F32, name="oT_ps")
+            nc.tensor.transpose(oT_ps[:], o[:], ident[:])
             return oT_ps
 
         def layer1(q, oT_ps):
-            oT = work.tile([P, CB, P], BF16, name="oT")
+            oT = work.tile([P, P], BF16, name="oT")
             nc.scalar.activation(oT[:], oT_ps[:], COPY)
-            bank = acc.tile([P, CB, H], F32, name="bank")
-            for cb in range(CB):
-                nc.tensor.matmul(bank[:, cb, :], oT[:, cb, :], w1_sb[:, q, :], start=True, stop=True)
+            bank = acc.tile([P, H], F32, name="bank")
+            nc.tensor.matmul(bank[:], oT[:], w1_sb[:, q, :], start=True, stop=True)
             return bank
 
-        def add_bias(bank, bias):
+        def add_bias(two_banks, bias):
             a = work.tile([P, CB, H], F32, name="a")
             for cb in range(CB):
-                nc.vector.tensor_tensor(a[:, cb, :], bank[:, cb, :], bias, ADD)
+                nc.vector.tensor_tensor(a[:, cb, :], two_banks[cb][:], bias, ADD)
             return a
 
         def times_slope(bank):
@@ -167,36 +166,39 @@ def tile_actor_dec_nw_kernel(tc, x, w1, b1, gain1, shift1, w2, b2, gain2, shift2
                 )
                 nc.sync.dma_start(out[cb * P : (cb + 1) * P, state_cols(q)], y[:, cb, :])
 
+        blocks = [(q, cb) for q in range(Q) for cb in range(CB)]
         flipped_o = {}
-        banks = {}
-        for q in range(Q + 1):
-            if q < Q:
-                flipped_o[q] = look_up_and_flip(q)
-            if q >= 1:
-                banks[q - 1] = layer1(q - 1, flipped_o[q - 1])
+        banks1 = {}
+        banks2 = {}
+        for i in range(len(blocks) + BEHIND):
+            if i < len(blocks):
+                flipped_o[blocks[i]] = look_up_and_flip(*blocks[i])
+            if i >= BEHIND:
+                q, cb = blocks[i - BEHIND]
+                banks1[q, cb] = layer1(q, flipped_o[q, cb])
 
         sloped = {}
         for j in range(2 * Q + 1):
             if j < Q:
-                a = add_bias(banks[j], b1_bc[:, state_cols(j)])
+                a = add_bias([banks1[j, cb] for cb in range(CB)], b1_bc[:, state_cols(j)])
             if j >= 1:
                 neg_mean = minus_mean(total)
                 previous = (v, neg_mean, rstd)
             if j < Q:
                 v, total, rstd = lrelu_and_spread(a, NEG_SLOPE, a)
             elif j < 2 * Q:
-                v, total, rstd = lrelu_and_spread(banks[j], 1.0, sloped[j])
+                v, total, rstd = lrelu_and_spread(banks2[j - Q], 1.0, sloped[j])
             if Q <= j + 1 < 2 * Q:
-                sloped[j + 1] = times_slope(banks[j + 1])
+                sloped[j + 1] = times_slope(banks2[j + 1 - Q])
             if j == 1:
-                rows_ps = flip_o.tile([P, CB, P], F32, name="rows_ps", tag="oT_ps")
-                nc.tensor.transpose(rows_ps[:, 0, :], rows[:], ident[:])
+                rows_ps = flip_o.tile([P, P], F32, name="rows_ps", tag="oT_ps")
+                nc.tensor.transpose(rows_ps[:], rows[:], ident[:])
                 cols1 = held.tile([P, 3 * Q * TB], F32, name="cols1")
-                nc.scalar.activation(cols1[:], rows_ps[:, 0, 0 : 3 * Q * TB], COPY)
+                nc.scalar.activation(cols1[:], rows_ps[:, 0 : 3 * Q * TB], COPY)
                 gain1_col = cols1[:, 0 : Q * TB]
                 shift1_col = cols1[:, Q * TB : 2 * Q * TB]
                 b2_col = cols1[:, 2 * Q * TB : 3 * Q * TB]
             if 1 <= j <= Q:
-                banks[Q + j - 1] = norm1_and_layer2(j - 1, *previous)
+                banks2[j - 1] = norm1_and_layer2(j - 1, *previous)
             elif j > Q:
                 norm2_and_store(j - 1 - Q, *previous)

@@ -12,10 +12,10 @@ P = 128
 C, S, Q, K, H, N = 256, 512, 4, 128, 256, 512
 CB = C // P
 TB = H // P
+UNITS = Q * CB
 NEG_SLOPE = 0.01
 EPS = 1e-5
 FLOPS = 2 * C * Q * (K * H + H * H)
-BEHIND = 2
 
 
 def state_cols(q):
@@ -27,10 +27,8 @@ def tile_actor_dec_nw_kernel(tc, x, w1, b1, gain1, shift1, w2, b2, gain2, shift2
     with (
         tc.tile_pool(name="held", bufs=1) as held,
         tc.tile_pool(name="work", bufs=4) as work,
-        tc.tile_pool(name="small", bufs=4) as small,
-        tc.psum_pool(name="flip_o", bufs=2) as flip_o,
-        tc.psum_pool(name="flip_n", bufs=2) as flip_n,
-        tc.psum_pool(name="acc", bufs=4) as acc,
+        tc.tile_pool(name="stats", bufs=6) as stats,
+        tc.psum_pool(name="psum", bufs=2) as psum,
     ):
         offsets = held.tile([P, N // 16], U16, name="offsets")
         x_blocks = [held.tile([P, S], F32, name=f"x_block{cb}") for cb in range(CB)]
@@ -60,145 +58,152 @@ def tile_actor_dec_nw_kernel(tc, x, w1, b1, gain1, shift1, w2, b2, gain2, shift2
         nc.vector.memset(eps[:], EPS)
         warm = held.tile([P, 1], F32, name="warm")
         nc.scalar.activation(warm[:], eps[:], RSQRT)
+        cols1 = held.tile([P, 3 * Q * TB], F32, name="cols1")
+        gain1_col = cols1[:, 0 : Q * TB]
+        shift1_col = cols1[:, Q * TB : 2 * Q * TB]
+        b2_col = cols1[:, 2 * Q * TB : 3 * Q * TB]
 
+        t = {}
 
-        def look_up_and_flip(q, cb):
+        def look_up(u, q, cb):
             o = work.tile([P, K], F32, name="o")
             piece = offsets[:, q * (K // 16) : (q + 1) * (K // 16)]
             nc.scalar.activation(o[:], x_blocks[cb][:].indirect(piece), COPY)
-            oT_ps = flip_o.tile([P, P], F32, name="oT_ps")
-            nc.tensor.transpose(oT_ps[:], o[:], ident[:])
-            return oT_ps
+            t["o", u] = o
 
-        def layer1(q, oT_ps):
+        def flip_o(u, q, cb):
+            oT_ps = psum.tile([P, P], F32, name="oT_ps")
+            nc.tensor.transpose(oT_ps[:], t["o", u][:], ident[:])
+            t["oT_ps", u] = oT_ps
+
+        def round_o(u, q, cb):
             oT = work.tile([P, P], BF16, name="oT")
-            nc.scalar.activation(oT[:], oT_ps[:], COPY)
-            bank = acc.tile([P, H], F32, name="bank")
-            nc.tensor.matmul(bank[:], oT[:], w1_sb[:, q, :], start=True, stop=True)
-            return bank
+            nc.scalar.activation(oT[:], t["oT_ps", u][:], COPY)
+            t["oT", u] = oT
 
-        def add_bias(two_banks, bias):
-            a = work.tile([P, CB, H], F32, name="a")
-            for cb in range(CB):
-                nc.vector.tensor_tensor(a[:, cb, :], two_banks[cb][:], bias, ADD)
-            return a
+        def layer1(u, q, cb):
+            bank1 = psum.tile([P, H], F32, name="bank1")
+            nc.tensor.matmul(bank1[:], t["oT", u][:], w1_sb[:, q, :], start=True, stop=True)
+            t["bank1", u] = bank1
 
-        def times_slope(bank):
-            sloped = work.tile([P, CB, H], F32, name="sloped")
-            nc.scalar.activation(sloped[:], bank[:], COPY, scale=NEG_SLOPE)
-            return sloped
+        def add_b1(u, q, cb):
+            a = work.tile([P, H], F32, name="a")
+            nc.vector.tensor_tensor(a[:], t["bank1", u][:], b1_bc[:, state_cols(q)], ADD)
+            t["a", u] = a
 
-        def lrelu_and_spread(a, slope, other):
-            v = work.tile([P, CB, H], F32, name="v")
-            total = small.tile([P, CB], F32, name="total")
-            for cb in range(CB):
-                nc.vector.scalar_tensor_tensor(
-                    v[:, cb, :], a[:, cb, :], slope, other[:, cb, :], MULT, MAX, accum_out=total[:, cb : cb + 1]
-                )
-            squares = work.tile([P, CB, H], F32, name="squares")
-            spread = small.tile([P, CB], F32, name="spread")
-            for cb in range(CB):
-                nc.scalar.activation(
-                    squares[:, cb, :],
-                    v[:, cb, :],
-                    SQUARE,
-                    bias=total[:, cb : cb + 1],
-                    scale=-float(H),
-                    accum_out=spread[:, cb : cb + 1],
-                )
-            rstd = small.tile([P, CB], F32, name="rstd")
-            nc.scalar.activation(rstd[:], spread[:], RSQRT, bias=eps[:], scale=1.0 / H**3)
-            return v, total, rstd
+        def lrelu1(u, q, cb):
+            v = stats.tile([P, H], F32, name="v1")
+            total = stats.tile([P, 1], F32, name="total1")
+            a = t["a", u]
+            nc.vector.scalar_tensor_tensor(v[:], a[:], NEG_SLOPE, a[:], MULT, MAX, accum_out=total[:])
+            t["v1", u], t["total1", u] = v, total
 
-        def minus_mean(total):
-            neg_mean = small.tile([P, CB], F32, name="neg_mean")
+        def spread(u, layer):
+            v, total = t["v" + layer, u], t["total" + layer, u]
+            squares = work.tile([P, H], F32, name="squares")
+            spread_sum = stats.tile([P, 1], F32, name="spread" + layer)
+            nc.scalar.activation(squares[:], v[:], SQUARE, bias=total[:], scale=-float(H), accum_out=spread_sum[:])
+            neg_mean = stats.tile([P, 1], F32, name="neg_mean" + layer)
             nc.vector.tensor_scalar(neg_mean[:], total[:], -1.0 / H, None, MULT)
-            return neg_mean
+            t["spread" + layer, u], t["neg_mean" + layer, u] = spread_sum, neg_mean
 
-        def norm1_and_layer2(q, v, neg_mean, rstd):
-            nT_ps = flip_n.tile([P, TB, CB, P], F32, name="nT_ps")
-            n = work.tile([P, CB, H], F32, name="n")
-            for cb in range(CB):
-                nc.vector.tensor_scalar(
-                    n[:, cb, :], v[:, cb, :], neg_mean[:, cb : cb + 1], rstd[:, cb : cb + 1], ADD, MULT
-                )
-                for tb in range(TB):
-                    nc.tensor.transpose(nT_ps[:, tb, cb, :], n[:, cb, tb * P : (tb + 1) * P], ident[:])
-            h1T = work.tile([P, TB, CB, P], BF16, name="h1T")
+        def inv_std(u, layer):
+            rstd = stats.tile([P, 1], F32, name="rstd" + layer)
+            nc.scalar.activation(rstd[:], t["spread" + layer, u][:], RSQRT, bias=eps[:], scale=1.0 / H**3)
+            t["rstd" + layer, u] = rstd
+
+        def spread1(u, q, cb):
+            spread(u, "1")
+
+        def inv_std1(u, q, cb):
+            inv_std(u, "1")
+
+        def norm1(u, q, cb):
+            n = work.tile([P, H], F32, name="n")
+            nc.vector.tensor_scalar(n[:], t["v1", u][:], t["neg_mean1", u][:], t["rstd1", u][:], ADD, MULT)
+            t["n", u] = n
+
+        def flip_n(u, q, cb):
+            if u == 0:
+                rows_ps = psum.tile([P, P], F32, name="rows_ps", tag="oT_ps")
+                nc.tensor.transpose(rows_ps[:], rows[:], ident[:])
+                nc.scalar.activation(cols1[:], rows_ps[:, 0 : 3 * Q * TB], COPY)
+            nT_ps = psum.tile([P, TB, P], F32, name="nT_ps")
+            for tb in range(TB):
+                nc.tensor.transpose(nT_ps[:, tb, :], t["n", u][:, tb * P : (tb + 1) * P], ident[:])
+            t["nT_ps", u] = nT_ps
+
+        def affine1(u, q, cb):
+            h1T = work.tile([P, TB, P], BF16, name="h1T")
             for tb in range(TB):
                 k = q * TB + tb
                 nc.scalar.activation(
-                    h1T[:, tb], nT_ps[:, tb], IDENTITY, bias=shift1_col[:, k : k + 1], scale=gain1_col[:, k : k + 1]
+                    h1T[:, tb, :],
+                    t["nT_ps", u][:, tb, :],
+                    IDENTITY,
+                    bias=shift1_col[:, k : k + 1],
+                    scale=gain1_col[:, k : k + 1],
                 )
-            bank = acc.tile([P, CB, H], F32, name="bank")
-            for cb in range(CB):
-                for ub in range(TB):
-                    k = q * TB + ub
-                    nc.tensor.matmul(
-                        bank[:, cb, ub * P : (ub + 1) * P],
-                        b2_col[:, k : k + 1].to_broadcast([P, P]),
-                        ident[:],
-                        is_transpose=True,
-                        start=(cb == 0 and ub == 0),
-                        stop=False,
-                    )
-            for cb in range(CB):
-                for tb in range(TB):
-                    nc.tensor.matmul(
-                        bank[:, cb, :],
-                        h1T[:, tb, cb, :],
-                        w2_sb[:, q * TB + tb, :],
-                        start=False,
-                        stop=(cb == CB - 1 and tb == TB - 1),
-                    )
-            return bank
+            t["h1T", u] = h1T
 
-        def norm2_and_store(q, v, neg_mean, rstd):
-            centred = work.tile([P, CB, H], F32, name="centred")
-            for cb in range(CB):
-                nc.vector.scalar_tensor_tensor(
-                    centred[:, cb, :], v[:, cb, :], neg_mean[:, cb : cb + 1], gain2_bc[:, state_cols(q)], ADD, MULT
+        def layer2(u, q, cb):
+            bank2 = psum.tile([P, H], F32, name="bank2")
+            for ub in range(TB):
+                k = q * TB + ub
+                nc.tensor.matmul(
+                    bank2[:, ub * P : (ub + 1) * P],
+                    b2_col[:, k : k + 1].to_broadcast([P, P]),
+                    ident[:],
+                    is_transpose=True,
+                    start=(ub == 0),
+                    stop=False,
                 )
-            y = work.tile([P, CB, H], F32, name="y")
-            for cb in range(CB):
-                nc.vector.scalar_tensor_tensor(
-                    y[:, cb, :], centred[:, cb, :], rstd[:, cb : cb + 1], shift2_bc[:, state_cols(q)], MULT, ADD
+            for tb in range(TB):
+                nc.tensor.matmul(
+                    bank2[:], t["h1T", u][:, tb, :], w2_sb[:, q * TB + tb, :], start=False, stop=(tb == TB - 1)
                 )
-                nc.sync.dma_start(out[cb * P : (cb + 1) * P, state_cols(q)], y[:, cb, :])
+            t["bank2", u] = bank2
 
-        blocks = [(q, cb) for q in range(Q) for cb in range(CB)]
-        flipped_o = {}
-        banks1 = {}
-        banks2 = {}
-        for i in range(len(blocks) + BEHIND):
-            if i < len(blocks):
-                flipped_o[blocks[i]] = look_up_and_flip(*blocks[i])
-            if i >= BEHIND:
-                q, cb = blocks[i - BEHIND]
-                banks1[q, cb] = layer1(q, flipped_o[q, cb])
+        def slope2(u, q, cb):
+            sloped = work.tile([P, H], F32, name="sloped")
+            nc.scalar.activation(sloped[:], t["bank2", u][:], COPY, scale=NEG_SLOPE)
+            t["sloped", u] = sloped
 
-        sloped = {}
-        for j in range(2 * Q + 1):
-            if j < Q:
-                a = add_bias([banks1[j, cb] for cb in range(CB)], b1_bc[:, state_cols(j)])
-            if j >= 1:
-                neg_mean = minus_mean(total)
-                previous = (v, neg_mean, rstd)
-            if j < Q:
-                v, total, rstd = lrelu_and_spread(a, NEG_SLOPE, a)
-            elif j < 2 * Q:
-                v, total, rstd = lrelu_and_spread(banks2[j - Q], 1.0, sloped[j])
-            if Q <= j + 1 < 2 * Q:
-                sloped[j + 1] = times_slope(banks2[j + 1 - Q])
-            if j == 1:
-                rows_ps = flip_o.tile([P, P], F32, name="rows_ps", tag="oT_ps")
-                nc.tensor.transpose(rows_ps[:], rows[:], ident[:])
-                cols1 = held.tile([P, 3 * Q * TB], F32, name="cols1")
-                nc.scalar.activation(cols1[:], rows_ps[:, 0 : 3 * Q * TB], COPY)
-                gain1_col = cols1[:, 0 : Q * TB]
-                shift1_col = cols1[:, Q * TB : 2 * Q * TB]
-                b2_col = cols1[:, 2 * Q * TB : 3 * Q * TB]
-            if 1 <= j <= Q:
-                banks2[j - 1] = norm1_and_layer2(j - 1, *previous)
-            elif j > Q:
-                norm2_and_store(j - 1 - Q, *previous)
+        def lrelu2(u, q, cb):
+            v = stats.tile([P, H], F32, name="v2")
+            total = stats.tile([P, 1], F32, name="total2")
+            nc.vector.scalar_tensor_tensor(
+                v[:], t["bank2", u][:], 1.0, t["sloped", u][:], MULT, MAX, accum_out=total[:]
+            )
+            t["v2", u], t["total2", u] = v, total
+
+        def spread2(u, q, cb):
+            spread(u, "2")
+
+        def inv_std2(u, q, cb):
+            inv_std(u, "2")
+
+        def centre2(u, q, cb):
+            centred = work.tile([P, H], F32, name="centred")
+            nc.vector.scalar_tensor_tensor(
+                centred[:], t["v2", u][:], t["neg_mean2", u][:], gain2_bc[:, state_cols(q)], ADD, MULT
+            )
+            t["centred", u] = centred
+
+        def finish2(u, q, cb):
+            y = work.tile([P, H], F32, name="y")
+            nc.vector.scalar_tensor_tensor(
+                y[:], t["centred", u][:], t["rstd2", u][:], shift2_bc[:, state_cols(q)], MULT, ADD
+            )
+            nc.sync.dma_start(out[cb * P : (cb + 1) * P, state_cols(q)], y[:])
+
+        stages = [
+            look_up, flip_o, round_o, layer1, add_b1, lrelu1, spread1, inv_std1, norm1, flip_n,
+            affine1, layer2, slope2, lrelu2, spread2, inv_std2, centre2, finish2,
+        ]
+
+        for step in range(UNITS + len(stages) - 1):
+            for k in reversed(range(len(stages))):
+                u = step - k
+                if 0 <= u < UNITS:
+                    stages[k](u, u // CB, u % CB)

@@ -164,17 +164,16 @@ def tile_actor_dec_nw_kernel(tc, x, w1, b1, gain1, shift1, w2, b2, gain2, shift2
                 )
             t["bank2", u] = bank2
 
-        def slope2(u, q, cb):
-            sloped = work.tile([P, H], F32, name="sloped")
-            nc.scalar.activation(sloped[:], t["bank2", u][:], COPY, scale=NEG_SLOPE)
-            t["sloped", u] = sloped
+        def copy_a2(u, q, cb):
+            a2 = work.tile([P, H], F32, name="a2")
+            nc.scalar.activation(a2[:], t["bank2", u][:], COPY)
+            t["a2", u] = a2
 
         def lrelu2(u, q, cb):
             v = stats.tile([P, H], F32, name="v2")
             total = stats.tile([P, 1], F32, name="total2")
-            nc.vector.scalar_tensor_tensor(
-                v[:], t["bank2", u][:], 1.0, t["sloped", u][:], MULT, MAX, accum_out=total[:]
-            )
+            a2 = t["a2", u]
+            nc.vector.scalar_tensor_tensor(v[:], a2[:], NEG_SLOPE, a2[:], MULT, MAX, accum_out=total[:])
             t["v2", u], t["total2", u] = v, total
 
         def spread2(u, q, cb):
@@ -197,9 +196,13 @@ def tile_actor_dec_nw_kernel(tc, x, w1, b1, gain1, shift1, w2, b2, gain2, shift2
             )
             nc.sync.dma_start(out[cb * P : (cb + 1) * P, state_cols(q)], y[:])
 
+        def inv_std2_and_centre2(u, q, cb):
+            centre2(u, q, cb)
+            inv_std2(u, q, cb)
+
         stages = [
             look_up, flip_o, round_o, layer1, add_b1, lrelu1, spread1, inv_std1, norm1, flip_n,
-            affine1, layer2, slope2, lrelu2, spread2, inv_std2, centre2, finish2,
+            affine1, layer2, copy_a2, lrelu2, spread2, inv_std2_and_centre2, finish2,
         ]
 
         for step in range(UNITS + len(stages) - 1):

@@ -16,6 +16,7 @@ UNITS = Q * CB
 NEG_SLOPE = 0.01
 EPS = 1e-5
 FLOPS = 2 * C * Q * (K * H + H * H)
+EARLY = 2
 
 
 def state_cols(q):
@@ -78,7 +79,10 @@ def tile_actor_dec_nw_kernel(tc, x, w1, b1, gain1, shift1, w2, b2, gain2, shift2
 
         def round_o(u, q, cb):
             oT = work.tile([P, P], BF16, name="oT")
-            nc.scalar.activation(oT[:], t["oT_ps", u][:], COPY)
+            if u < EARLY:
+                nc.vector.tensor_copy(oT[:], t["oT_ps", u][:])
+            else:
+                nc.scalar.activation(oT[:], t["oT_ps", u][:], COPY)
             t["oT", u] = oT
 
         def layer1(u, q, cb):

@@ -55,6 +55,8 @@ def tile_actor_dec_nw_kernel(tc, x, w1, b1, gain1, shift1, w2, b2, gain2, shift2
 
         ident = held.tile([P, P], F32, name="ident")
         make_identity(nc, ident[:])
+        ident_bf = held.tile([P, P], BF16, name="ident_bf")
+        make_identity(nc, ident_bf[:])
         eps = held.tile([P, 1], F32, name="eps")
         nc.vector.memset(eps[:], EPS)
         warm = held.tile([P, 1], F32, name="warm")
@@ -73,8 +75,9 @@ def tile_actor_dec_nw_kernel(tc, x, w1, b1, gain1, shift1, w2, b2, gain2, shift2
             t["o", u] = o
 
         def flip_o(u, q, cb):
-            oT_ps = psum.tile([P, P], F32, name="oT_ps")
-            nc.tensor.transpose(oT_ps[:], t["o", u][:], ident[:])
+            oT_ps = psum.tile([P, P], BF16, name="oT_ps")
+            o_bf = t["o", u][:].bitcast(BF16)[:, 1::2]
+            nc.tensor.transpose(oT_ps[:], o_bf, ident_bf[:])
             t["oT_ps", u] = oT_ps
 
         def round_o(u, q, cb):

@@ -44,8 +44,11 @@ def tile_actor_dec_nw_kernel(tc, x, w1, b1, gain1, shift1, w2, b2, gain2, shift2
         nc.sync.dma_start(offsets[:], offs)
         nc.scalar.dma_start(x_blocks[0][:], x[0:P, :])
         nc.sync.dma_start(x_blocks[1][:], x[P : 2 * P, :])
+        for q in range(Q):
+            nc.sync.dma_start(
+                b1_bc[:, state_cols(q)], b1[:, state_cols(q)].rearrange("o n -> (o n)").partition_broadcast(P)
+            )
         nc.scalar.dma_start(w1_sb[:], w1.rearrange("(q i) t -> i q t", i=P))
-        nc.sync.dma_start(b1_bc[:], b1.rearrange("o n -> (o n)").partition_broadcast(P))
         nc.sync.dma_start(rows[0 : Q * TB, :], gain1.rearrange("o (k t) -> (o k) t", t=P))
         nc.sync.dma_start(rows[Q * TB : 2 * Q * TB, :], shift1.rearrange("o (k t) -> (o k) t", t=P))
         nc.sync.dma_start(rows[2 * Q * TB : 3 * Q * TB, :], b2.rearrange("o (k t) -> (o k) t", t=P))

@@ -80,7 +80,7 @@ def tile_actor_dec_nw_kernel(tc, x, w1, b1, gain1, shift1, w2, b2, gain2, shift2
         def flip_o(u, q, cb):
             oT_ps = psum.tile([P, P], BF16, name="oT_ps")
             o_bf = t["o", u][:].bitcast(BF16)[:, 1::2]
-            nc.tensor.transpose(oT_ps[:], o_bf, ident_bf[:])
+            nc.tensor.matmul(oT_ps[:], o_bf, ident_bf[:], start=True, stop=True)
             t["oT_ps", u] = oT_ps
 
         def round_o(u, q, cb):

@@ -114,7 +114,8 @@ def tile_actor_dec_nw_kernel(tc, x, w1, b1, gain1, shift1, w2, b2, gain2, shift2
             spread_sum = stats.tile([P, 1], F32, name="spread" + layer)
             nc.scalar.activation(squares[:], v[:], SQUARE, bias=total[:], scale=-float(H), accum_out=spread_sum[:])
             neg_mean = stats.tile([P, 1], F32, name="neg_mean" + layer)
-            nc.vector.tensor_scalar(neg_mean[:], total[:], -1.0 / H, None, MULT)
+            neg_mean_engine = nc.gpsimd if layer == "1" else nc.vector
+            neg_mean_engine.tensor_scalar(neg_mean[:], total[:], -1.0 / H, None, MULT)
             t["spread" + layer, u], t["neg_mean" + layer, u] = spread_sum, neg_mean
 
         def inv_std(u, layer):
@@ -201,10 +202,14 @@ def tile_actor_dec_nw_kernel(tc, x, w1, b1, gain1, shift1, w2, b2, gain2, shift2
 
         def finish2(u, q, cb):
             y = work.tile([P, H], F32, name="y")
-            nc.vector.scalar_tensor_tensor(
-                y[:], t["centred", u][:], t["rstd2", u][:], shift2_bc[:, state_cols(q)], MULT, ADD
-            )
-            nc.sync.dma_start(out[cb * P : (cb + 1) * P, state_cols(q)], y[:])
+            width = H // 2 if u == UNITS - 1 else H
+            for first in range(0, H, width):
+                half = slice(first, first + width)
+                columns = slice(q * H + first, q * H + first + width)
+                nc.vector.scalar_tensor_tensor(
+                    y[:, half], t["centred", u][:, half], t["rstd2", u][:], shift2_bc[:, columns], MULT, ADD
+                )
+                nc.sync.dma_start(out[cb * P : (cb + 1) * P, columns], y[:, half])
 
         def inv_std2_and_centre2(u, q, cb):
             centre2(u, q, cb)

@@ -202,14 +202,10 @@ def tile_actor_dec_nw_kernel(tc, x, w1, b1, gain1, shift1, w2, b2, gain2, shift2
 
         def finish2(u, q, cb):
             y = work.tile([P, H], F32, name="y")
-            width = H // 2 if u == UNITS - 1 else H
-            for first in range(0, H, width):
-                half = slice(first, first + width)
-                columns = slice(q * H + first, q * H + first + width)
-                nc.vector.scalar_tensor_tensor(
-                    y[:, half], t["centred", u][:, half], t["rstd2", u][:], shift2_bc[:, columns], MULT, ADD
-                )
-                nc.sync.dma_start(out[cb * P : (cb + 1) * P, columns], y[:, half])
+            nc.vector.scalar_tensor_tensor(
+                y[:], t["centred", u][:], t["rstd2", u][:], shift2_bc[:, state_cols(q)], MULT, ADD
+            )
+            nc.sync.dma_start(out[cb * P : (cb + 1) * P, state_cols(q)], y[:])
 
         def inv_std2_and_centre2(u, q, cb):
             centre2(u, q, cb)

import concourse.mybir as mybir
from concourse.masks import make_identity

F32, BF16, U16 = mybir.dt.float32, mybir.dt.bfloat16, mybir.dt.uint16
ADD, MULT, MAX = mybir.AluOpType.add, mybir.AluOpType.mult, mybir.AluOpType.max
COPY = mybir.ActivationFunctionType.Copy
IDENTITY = mybir.ActivationFunctionType.Identity
SQUARE = mybir.ActivationFunctionType.Square
RSQRT = mybir.ActivationFunctionType.Abs_reciprocal_sqrt

P = 128
C, S, Q, K, H, N = 256, 512, 4, 128, 256, 512
CB = C // P
TB = H // P
UNITS = Q * CB
NEG_SLOPE = 0.01
EPS = 1e-5
FLOPS = 2 * C * Q * (K * H + H * H)
EARLY = 2


def state_cols(q):
    return slice(q * H, (q + 1) * H)


def tile_actor_dec_nw_kernel(tc, x, w1, b1, gain1, shift1, w2, b2, gain2, shift2, offs, out):
    nc = tc.nc
    with (
        tc.tile_pool(name="held", bufs=1) as held,
        tc.tile_pool(name="work", bufs=4) as work,
        tc.tile_pool(name="stats", bufs=6) as stats,
        tc.psum_pool(name="psum", bufs=2) as psum,
    ):
        offsets = held.tile([P, N // 16], U16, name="offsets")
        x_blocks = [held.tile([P, S], F32, name=f"x_block{cb}") for cb in range(CB)]
        w1_sb = held.tile([P, Q, H], BF16, name="w1_sb")
        w2_sb = held.tile([P, Q * TB, H], BF16, name="w2_sb")
        b1_bc = held.tile([P, Q * H], F32, name="b1_bc")
        gain2_bc = held.tile([P, Q * H], F32, name="gain2_bc")
        shift2_bc = held.tile([P, Q * H], F32, name="shift2_bc")
        rows = held.tile([P, P], F32, name="rows")
        nc.vector.memset(rows[:], 0.0)

        nc.sync.dma_start(offsets[:], offs)
        nc.scalar.dma_start(x_blocks[0][:], x[0:P, :])
        nc.sync.dma_start(x_blocks[1][:], x[P : 2 * P, :])
        for q in range(Q):
            nc.sync.dma_start(
                b1_bc[:, state_cols(q)], b1[:, state_cols(q)].rearrange("o n -> (o n)").partition_broadcast(P)
            )
        nc.scalar.dma_start(w1_sb[:], w1.rearrange("(q i) t -> i q t", i=P))
        nc.sync.dma_start(rows[0 : Q * TB, :], gain1.rearrange("o (k t) -> (o k) t", t=P))
        nc.sync.dma_start(rows[Q * TB : 2 * Q * TB, :], shift1.rearrange("o (k t) -> (o k) t", t=P))
        nc.sync.dma_start(rows[2 * Q * TB : 3 * Q * TB, :], b2.rearrange("o (k t) -> (o k) t", t=P))
        nc.sync.dma_start(w2_sb[:], w2.rearrange("(k t) u -> t k u", t=P))
        nc.sync.dma_start(gain2_bc[:], gain2.rearrange("o n -> (o n)").partition_broadcast(P))
        nc.sync.dma_start(shift2_bc[:], shift2.rearrange("o n -> (o n)").partition_broadcast(P))

        ident = held.tile([P, P], F32, name="ident")
        make_identity(nc, ident[:])
        ident_bf = held.tile([P, P], BF16, name="ident_bf")
        make_identity(nc, ident_bf[:])
        eps = held.tile([P, 1], F32, name="eps")
        nc.vector.memset(eps[:], EPS)
        warm = held.tile([P, 1], F32, name="warm")
        nc.scalar.activation(warm[:], eps[:], RSQRT)
        cols1 = held.tile([P, 3 * Q * TB], F32, name="cols1")
        gain1_col = cols1[:, 0 : Q * TB]
        shift1_col = cols1[:, Q * TB : 2 * Q * TB]
        b2_col = cols1[:, 2 * Q * TB : 3 * Q * TB]

        t = {}

        def look_up(u, q, cb):
            o = work.tile([P, K], F32, name="o")
            piece = offsets[:, q * (K // 16) : (q + 1) * (K // 16)]
            nc.scalar.activation(o[:], x_blocks[cb][:].indirect(piece), COPY)
            t["o", u] = o

        def flip_o(u, q, cb):
            oT_ps = psum.tile([P, P], BF16, name="oT_ps")
            o_bf = t["o", u][:].bitcast(BF16)[:, 1::2]
            nc.tensor.matmul(oT_ps[:], o_bf, ident_bf[:], start=True, stop=True)
            t["oT_ps", u] = oT_ps

        def round_o(u, q, cb):
            oT = work.tile([P, P], BF16, name="oT")
            if u < EARLY:
                nc.vector.tensor_copy(oT[:], t["oT_ps", u][:])
            else:
                nc.scalar.activation(oT[:], t["oT_ps", u][:], COPY)
            t["oT", u] = oT

        def layer1(u, q, cb):
            bank1 = psum.tile([P, H], F32, name="bank1")
            nc.tensor.matmul(bank1[:], t["oT", u][:], w1_sb[:, q, :], start=True, stop=True)
            t["bank1", u] = bank1

        def add_b1(u, q, cb):
            a = work.tile([P, H], F32, name="a")
            nc.vector.tensor_tensor(a[:], t["bank1", u][:], b1_bc[:, state_cols(q)], ADD)
            t["a", u] = a

        def lrelu1(u, q, cb):
            v = stats.tile([P, H], F32, name="v1")
            total = stats.tile([P, 1], F32, name="total1")
            a = t["a", u]
            nc.vector.scalar_tensor_tensor(v[:], a[:], NEG_SLOPE, a[:], MULT, MAX, accum_out=total[:])
            t["v1", u], t["total1", u] = v, total

        def spread(u, layer):
            v, total = t["v" + layer, u], t["total" + layer, u]
            squares = work.tile([P, H], F32, name="squares")
            spread_sum = stats.tile([P, 1], F32, name="spread" + layer)
            nc.scalar.activation(squares[:], v[:], SQUARE, bias=total[:], scale=-float(H), accum_out=spread_sum[:])
            neg_mean = stats.tile([P, 1], F32, name="neg_mean" + layer)
            neg_mean_engine = nc.gpsimd if layer == "1" else nc.vector
            neg_mean_engine.tensor_scalar(neg_mean[:], total[:], -1.0 / H, None, MULT)
            t["spread" + layer, u], t["neg_mean" + layer, u] = spread_sum, neg_mean

        def inv_std(u, layer):
            rstd = stats.tile([P, 1], F32, name="rstd" + layer)
            nc.scalar.activation(rstd[:], t["spread" + layer, u][:], RSQRT, bias=eps[:], scale=1.0 / H**3)
            t["rstd" + layer, u] = rstd

        def spread1(u, q, cb):
            spread(u, "1")

        def inv_std1(u, q, cb):
            inv_std(u, "1")

        def norm1(u, q, cb):
            n = work.tile([P, H], F32, name="n")
            nc.vector.tensor_scalar(n[:], t["v1", u][:], t["neg_mean1", u][:], t["rstd1", u][:], ADD, MULT)
            t["n", u] = n

        def flip_n(u, q, cb):
            if u == 0:
                rows_ps = psum.tile([P, P], F32, name="rows_ps", tag="oT_ps")
                nc.tensor.transpose(rows_ps[:], rows[:], ident[:])
                nc.scalar.activation(cols1[:], rows_ps[:, 0 : 3 * Q * TB], COPY)
            nT_ps = psum.tile([P, TB, P], F32, name="nT_ps")
            for tb in range(TB):
                nc.tensor.transpose(nT_ps[:, tb, :], t["n", u][:, tb * P : (tb + 1) * P], ident[:])
            t["nT_ps", u] = nT_ps

        def affine1(u, q, cb):
            h1T = work.tile([P, TB, P], BF16, name="h1T")
            for tb in range(TB):
                k = q * TB + tb
                nc.scalar.activation(
                    h1T[:, tb, :],
                    t["nT_ps", u][:, tb, :],
                    IDENTITY,
                    bias=shift1_col[:, k : k + 1],
                    scale=gain1_col[:, k : k + 1],
                )
            t["h1T", u] = h1T

        def layer2(u, q, cb):
            bank2 = psum.tile([P, H], F32, name="bank2")
            for ub in range(TB):
                k = q * TB + ub
                nc.tensor.matmul(
                    bank2[:, ub * P : (ub + 1) * P],
                    b2_col[:, k : k + 1].to_broadcast([P, P]),
                    ident[:],
                    is_transpose=True,
                    start=(ub == 0),
                    stop=False,
                )
            for tb in range(TB):
                nc.tensor.matmul(
                    bank2[:], t["h1T", u][:, tb, :], w2_sb[:, q * TB + tb, :], start=False, stop=(tb == TB - 1)
                )
            t["bank2", u] = bank2

        def copy_a2(u, q, cb):
            a2 = work.tile([P, H], F32, name="a2")
            nc.scalar.activation(a2[:], t["bank2", u][:], COPY)
            t["a2", u] = a2

        def lrelu2(u, q, cb):
            v = stats.tile([P, H], F32, name="v2")
            total = stats.tile([P, 1], F32, name="total2")
            a2 = t["a2", u]
            nc.vector.scalar_tensor_tensor(v[:], a2[:], NEG_SLOPE, a2[:], MULT, MAX, accum_out=total[:])
            t["v2", u], t["total2", u] = v, total

        def spread2(u, q, cb):
            spread(u, "2")

        def inv_std2(u, q, cb):
            inv_std(u, "2")

        def centre2(u, q, cb):
            centred = work.tile([P, H], F32, name="centred")
            nc.vector.scalar_tensor_tensor(
                centred[:], t["v2", u][:], t["neg_mean2", u][:], gain2_bc[:, state_cols(q)], ADD, MULT
            )
            t["centred", u] = centred

        def finish2(u, q, cb):
            y = work.tile([P, H], F32, name="y")
            nc.vector.scalar_tensor_tensor(
                y[:], t["centred", u][:], t["rstd2", u][:], shift2_bc[:, state_cols(q)], MULT, ADD
            )
            nc.sync.dma_start(out[cb * P : (cb + 1) * P, state_cols(q)], y[:])

        def inv_std2_and_centre2(u, q, cb):
            centre2(u, q, cb)
            inv_std2(u, q, cb)

        stages = [
            look_up, flip_o, round_o, layer1, add_b1, lrelu1, spread1, inv_std1, norm1, flip_n,
            affine1, layer2, copy_a2, lrelu2, spread2, inv_std2_and_centre2, finish2,
        ]

        for step in range(UNITS + len(stages) - 1):
            for k in reversed(range(len(stages))):
                u = step - k
                if 0 <= u < UNITS:
                    stages[k](u, u // CB, u % CB)
